import numpy as np
import ml_dtypes


def mxq(x, axis, fmt="e4m3"):
    dtype, down = {"e4m3": (ml_dtypes.float8_e4m3fn, 7), "e5m2": (ml_dtypes.float8_e5m2, 14)}[fmt]
    v = np.moveaxis(np.asarray(x, np.float32).astype(ml_dtypes.bfloat16).astype(np.float64), axis, -1)
    blocks = v.reshape(v.shape[:-1] + (-1, 32))
    amax = np.abs(blocks).max(-1, keepdims=True)
    byte = np.maximum(np.where(amax > 0, np.frexp(amax)[1] - 1 + 127, 0) - down, 1)
    scale = np.exp2(byte - 127.0)
    codes = (blocks / scale).astype(np.float32).astype(dtype).astype(np.float64)
    return np.moveaxis((codes * scale).reshape(v.shape), -1, axis)


WIDE = False


def mx_kscale(k):
    if not WIDE:
        return np.ones(k)
    levels = np.array([10, -10, 5, -5, 0])
    a = np.random.permutation(np.resize(levels, k // 512 * 4)).reshape(k // 512, 4)
    idx = np.arange(k)
    return np.exp2(a[idx // 512, idx % 128 // 32])


BF16 = ml_dtypes.bfloat16


def bf(x):
    return np.asarray(x, np.float32).astype(BF16)


def f64(x):
    return np.asarray(x).astype(np.float64)


B, S, D, QR, KR, H, NOPE, ROPE, VD = 2, 64, 1024, 1536, 512, 16, 64, 64, 64
EPS = 1e-6
THETA = 10000.0
LAT = 3.0 * np.sqrt(EPS)


def rmsnorm(x, w):
    var = np.mean(x * x, axis=-1, keepdims=True)
    return w * (x * (1.0 / np.sqrt(var + EPS)))


def rope_cos_sin(seq_len):
    inv_freq = 1.0 / (THETA ** (f64(np.arange(0, ROPE, 2)) / ROPE))
    t = f64(np.arange(seq_len))
    freqs = np.outer(t, inv_freq)
    emb = np.concatenate([freqs, freqs], -1)
    return np.cos(emb), np.sin(emb)


def rotate_half(x):
    x1, x2 = x[..., : x.shape[-1] // 2], x[..., x.shape[-1] // 2 :]
    return np.concatenate([-x2, x1], axis=-1)


def setup_inputs():
    s, t = mx_kscale(D), mx_kscale(KR)
    return {"hidden_states": bf(np.random.standard_normal((B, S, D)) * s),
            "kv_a_w_ckv": bf(np.random.standard_normal((KR, D)) * LAT / np.sqrt(D) / s[None, :]),
            "k_pe_raw": bf(np.random.standard_normal((B, S, ROPE))),
            "kv_a_ln_w": bf((1.0 + 0.1 * np.random.standard_normal(KR)) * t),
            "kv_b_w": bf(np.random.standard_normal((H * (NOPE + VD), KR)) / np.sqrt(KR) / t[None, :])}


def reference(hidden_states, kv_a_w_ckv, k_pe_raw, kv_a_ln_w, kv_b_w):
    ckv = mxq(f64(hidden_states), 2, "e4m3") @ mxq(f64(kv_a_w_ckv), 1, "e4m3").T
    ckv_n = rmsnorm(ckv, f64(kv_a_ln_w))
    kv = mxq(ckv_n, 2, "e4m3") @ mxq(f64(kv_b_w), 1, "e4m3").T
    kv = kv.reshape(B, S, H, NOPE + VD).transpose(0, 2, 1, 3)
    k_nope, v = kv[..., :NOPE], kv[..., NOPE:]
    k_pe = f64(k_pe_raw).reshape(B, 1, S, ROPE)
    cos, sin = rope_cos_sin(S)
    cos, sin = cos[None, None], sin[None, None]
    k_pe = k_pe * cos + rotate_half(k_pe) * sin
    key_s = np.concatenate([k_nope, np.broadcast_to(k_pe, (B, H, S, ROPE))], -1)
    return key_s, v

@@ -1,0 +1,268 @@
+import math
+from contextlib import ExitStack
+
+import concourse.mybir as mybir
+from concourse.masks import make_identity
+
+F32 = mybir.dt.float32
+BF16 = mybir.dt.bfloat16
+U32 = mybir.dt.uint32
+U8 = mybir.dt.uint8
+FP8X4 = mybir.dt.float8_e4m3fn_x4
+ACT = mybir.ActivationFunctionType
+ALU = mybir.AluOpType
+
+P = 128
+PACK = 4
+BATCH, SEQ = 2, 64
+TOK = BATCH * SEQ
+D = 1024
+KR = 512
+HEADS, HEAD_COLS, HALF_HEAD = 16, 128, 64
+ROPE, ROPE_HALF = 64, 32
+PASSES_1 = D // (P * PACK)
+CHUNKS = KR // P
+QUARTERS = 4
+QUARTER_ROWS = HEADS * HEAD_COLS // QUARTERS
+HEADS_PER_QUARTER = HEADS // QUARTERS
+EPS = 1e-6
+THETA = 10000.0
+ROUND_MAGIC = 12582912.0
+
+FLOPS = 2 * TOK * D * KR + 2 * TOK * KR * HEADS * HEAD_COLS
+
+
+def transpose_words(nc, bank, rows_bf16, ident):
+    words = rows_bf16.bitcast(F32)
+    for u in range(2):
+        nc.tensor.transpose(bank[:, u, :], words[:, P * u : P * (u + 1)], ident)
+
+
+def tile_modelnew_pb_s_kernel(
+    tc, hidden_states, kv_a_w_ckv, k_pe_raw, kv_a_ln_w, kv_b_w, key_s, v
+):
+    nc = tc.nc
+    with ExitStack() as ctx:
+        keep = ctx.enter_context(tc.tile_pool(name="keep", bufs=1))
+        staging = ctx.enter_context(tc.psum_pool(name="staging", bufs=3))
+        products = ctx.enter_context(tc.psum_pool(name="products", bufs=4))
+        norm_psum = ctx.enter_context(tc.psum_pool(name="norm_psum", bufs=1))
+
+        x_sb = keep.tile([P, D], BF16)
+        nc.sync.dma_start(out=x_sb[:], in_=hidden_states.flatten_outer_dims())
+        wa_sb = keep.tile([P, CHUNKS, D], BF16)
+        wa_rows = kv_a_w_ckv.rearrange("(u p e) k -> u e p k", u=2, e=2)
+        for t in range(CHUNKS):
+            nc.sync.dma_start(out=wa_sb[:, t, :], in_=wa_rows[t // 2, t % 2])
+        wb_sb = keep.tile([P, QUARTERS, PACK, KR], BF16)
+        wb_rows = kv_b_w.rearrange("(q p i) k -> q p i k", q=QUARTERS, i=PACK)
+        for q in range(QUARTERS):
+            nc.sync.dma_start(out=wb_sb[:, q], in_=wb_rows[q])
+        pe_sb = keep.tile([P, ROPE], BF16)
+        nc.scalar.dma_start(out=pe_sb[:], in_=k_pe_raw.flatten_outer_dims())
+        gain_bf = keep.tile([P, 2, 2], BF16)
+        nc.scalar.dma_start(out=gain_bf[:], in_=kv_a_ln_w.rearrange("(u p e) -> p u e", u=2, e=2))
+
+        ident = keep.tile([P, P], F32)
+        make_identity(nc, ident[:])
+        ones = keep.tile([P, P], F32)
+        nc.gpsimd.memset(ones[:], 1.0)
+        pos = keep.tile([P, 1], F32)
+        for b in range(BATCH):
+            nc.gpsimd.iota(
+                pos[SEQ * b : SEQ * (b + 1), :],
+                pattern=[[0, 1]],
+                base=0,
+                channel_multiplier=1,
+                allow_small_or_imprecise_dtypes=True,
+            )
+
+        freq = keep.tile([P, 2, ROPE_HALF], F32)
+        nc.vector.memset(freq[:, :, 0:1], 1.0)
+        for step in range(5):
+            w = 2**step
+            nc.vector.tensor_scalar(
+                out=freq[:, :, w : 2 * w],
+                in0=freq[:, :, 0:w],
+                scalar1=THETA ** (-w / ROPE_HALF),
+                scalar2=None,
+                op0=ALU.mult,
+            )
+        eps = keep.tile([P, 1], F32)
+        nc.vector.tensor_scalar(
+            out=eps[:], in0=freq[:, 0, 0:1], scalar1=EPS, scalar2=None, op0=ALU.mult
+        )
+        turns = keep.tile([P, 2, ROPE_HALF], F32)
+        nc.vector.tensor_scalar(
+            out=turns[:],
+            in0=freq[:],
+            scalar1=pos[:, 0:1],
+            scalar2=1.0 / (2.0 * math.pi),
+            op0=ALU.mult,
+            op1=ALU.mult,
+        )
+        nc.vector.tensor_scalar_add(out=turns[:, 1, :], in0=turns[:, 1, :], scalar1=0.25)
+        whole = keep.tile([P, 2, ROPE_HALF], F32)
+        nc.vector.tensor_scalar(
+            out=whole[:],
+            in0=turns[:],
+            scalar1=ROUND_MAGIC,
+            scalar2=ROUND_MAGIC,
+            op0=ALU.add,
+            op1=ALU.subtract,
+        )
+        frac = keep.tile([P, 2, ROPE_HALF], F32)
+        nc.vector.tensor_tensor(out=frac[:], in0=turns[:], in1=whole[:], op=ALU.subtract)
+        sin_cos = keep.tile([P, 2, ROPE_HALF], F32)
+        nc.scalar.activation(out=sin_cos[:], in_=frac[:], func=ACT.Sin, scale=2.0 * math.pi)
+        table_warm = keep.tile([P, 1], F32)
+        nc.scalar.activation(out=table_warm[:], in_=sin_cos[:, 1, 0:1], func=ACT.Abs_reciprocal_sqrt)
+
+        prod = keep.tile([P, 2, 2, ROPE_HALF], F32)
+        nc.gpsimd.tensor_tensor(
+            out=prod[:],
+            in0=pe_sb[:].rearrange("p (h j) -> p h j", h=2).unsqueeze(1).to_broadcast([P, 2, 2, ROPE_HALF]),
+            in1=sin_cos[:].unsqueeze(2).to_broadcast([P, 2, 2, ROPE_HALF]),
+            op=ALU.mult,
+        )
+        rope = keep.tile([P, ROPE], F32)
+        nc.gpsimd.tensor_tensor(
+            out=rope[:, 0:ROPE_HALF], in0=prod[:, 1, 0, :], in1=prod[:, 0, 1, :], op=ALU.subtract
+        )
+        nc.gpsimd.tensor_tensor(
+            out=rope[:, ROPE_HALF:ROPE], in0=prod[:, 1, 1, :], in1=prod[:, 0, 0, :], op=ALU.add
+        )
+        gain = keep.tile([P, CHUNKS], F32)
+        nc.gpsimd.tensor_copy(out=gain[:], in_=gain_bf[:].rearrange("p u e -> p (u e)"))
+
+        x_bank = staging.tile([P, PASSES_1, 2, TOK], F32, tag="bank")
+        for g in range(PASSES_1):
+            transpose_words(nc, x_bank[:, g], x_sb[:, KR * g : KR * (g + 1)], ident[:])
+        x_grouped = keep.tile([P, PASSES_1, TOK, PACK], BF16, align_bytes=64)
+        nc.vector.tensor_copy(
+            out=x_grouped[:].bitcast(F32), in_=x_bank[:].rearrange("p g u r -> p g r u")
+        )
+        x_codes = keep.tile([P, PASSES_1, TOK], U32, align_bytes=64)
+        x_scales = keep.tile([P, PASSES_1, TOK], U8, align_bytes=64)
+        nc.vector.quantize_mx(
+            out=x_codes[:].rearrange("p g r -> p (g r)").bitcast(FP8X4),
+            scales=x_scales[:].rearrange("p g r -> p (g r)"),
+            in_=x_grouped[:].rearrange("p g r k -> p (g r k)"),
+        )
+
+        wa_grouped = keep.tile([P, CHUNKS, PASSES_1, P, PACK], BF16, align_bytes=64)
+        wa_codes = keep.tile([P, CHUNKS, PASSES_1, P], U32, align_bytes=64)
+        wa_scales = keep.tile([P, CHUNKS, PASSES_1, P], U8, align_bytes=64)
+        squares = keep.tile([P, CHUNKS, TOK], F32)
+        gained = keep.tile([P, CHUNKS, TOK], F32)
+        sum_sq = norm_psum.tile([P, TOK], F32)
+        for t in range(CHUNKS):
+            wa_bank = staging.tile([P, PASSES_1, 2, P], F32, tag="bank")
+            for g in range(PASSES_1):
+                transpose_words(nc, wa_bank[:, g], wa_sb[:, t, KR * g : KR * (g + 1)], ident[:])
+            copy_out = nc.scalar.copy if t % 2 == 0 else nc.vector.tensor_copy
+            copy_out(
+                out=wa_grouped[:, t].bitcast(F32), in_=wa_bank[:].rearrange("p g u m -> p g m u")
+            )
+            nc.vector.quantize_mx(
+                out=wa_codes[:, t].rearrange("p g m -> p (g m)").bitcast(FP8X4),
+                scales=wa_scales[:, t].rearrange("p g m -> p (g m)"),
+                in_=wa_grouped[:, t].rearrange("p g m k -> p (g m k)"),
+            )
+            ckv_t = products.tile([P, TOK], F32, tag="product")
+            for g in range(PASSES_1):
+                nc.tensor.matmul_mx(
+                    out=ckv_t[:],
+                    lhsT=wa_codes[:, t, g, :].bitcast(FP8X4),
+                    lhsT_scale=wa_scales[:, t, g, :],
+                    rhs=x_codes[:, g, :].bitcast(FP8X4),
+                    rhs_scale=x_scales[:, g, :],
+                    start=(g == 0),
+                    stop=(g == PASSES_1 - 1),
+                )
+            nc.scalar.activation(out=squares[:, t, :], in_=ckv_t[:], func=ACT.Square)
+            nc.scalar.activation(
+                out=gained[:, t, :], in_=ckv_t[:], func=ACT.Copy, scale=gain[:, t : t + 1]
+            )
+            nc.tensor.matmul(
+                out=sum_sq[:],
+                lhsT=ones[:],
+                rhs=squares[:, t, :],
+                start=(t == 0),
+                stop=(t == CHUNKS - 1),
+            )
+
+        rstd = keep.tile([P, TOK], F32)
+        nc.scalar.activation(
+            out=rstd[:], in_=sum_sq[:], func=ACT.Abs_reciprocal_sqrt, bias=eps[:, 0:1], scale=1.0 / KR
+        )
+        cn_grouped = keep.tile([P, TOK, PACK], BF16, align_bytes=64)
+        nc.vector.tensor_tensor(
+            out=cn_grouped[:],
+            in0=gained[:].rearrange("p t r -> p r t"),
+            in1=rstd[:].unsqueeze(2).to_broadcast([P, TOK, PACK]),
+            op=ALU.mult,
+        )
+        cn_codes = keep.tile([P, TOK], U32, align_bytes=64)
+        cn_scales = keep.tile([P, TOK], U8, align_bytes=64)
+        nc.vector.quantize_mx(
+            out=cn_codes[:].bitcast(FP8X4),
+            scales=cn_scales[:],
+            in_=cn_grouped[:].rearrange("p r k -> p (r k)"),
+        )
+
+        for b in range(BATCH):
+            nc.sync.dma_start(
+                out=key_s[b].rearrange("h s d -> s h d")[:, :, HALF_HEAD:HEAD_COLS],
+                in_=rope[SEQ * b : SEQ * (b + 1), :].unsqueeze(1).to_broadcast([SEQ, HEADS, ROPE]),
+            )
+
+        wb_grouped = keep.tile([P, QUARTERS, 2, 2 * P, PACK], BF16, align_bytes=64)
+        wb_codes = keep.tile([P, QUARTERS, QUARTER_ROWS], U32, align_bytes=64)
+        wb_scales = keep.tile([P, QUARTERS, QUARTER_ROWS], U8, align_bytes=64)
+        kv_sb = keep.tile([P, HEADS * HEAD_COLS], F32)
+        for q in range(QUARTERS):
+            for half in range(2):
+                wb_bank = staging.tile([P, 2, 2, P], F32, tag="bank")
+                for j in range(2):
+                    transpose_words(nc, wb_bank[:, j], wb_sb[:, q, 2 * half + j, :], ident[:])
+                copy_out = nc.scalar.copy if half == 0 else nc.vector.tensor_copy
+                copy_out(
+                    out=wb_grouped[:, q, half].bitcast(F32).rearrange("p (j n) u -> p j n u", j=2),
+                    in_=wb_bank[:].rearrange("p j u n -> p j n u"),
+                )
+                cols = slice(2 * P * half, 2 * P * (half + 1))
+                nc.vector.quantize_mx(
+                    out=wb_codes[:, q, cols].bitcast(FP8X4),
+                    scales=wb_scales[:, q, cols],
+                    in_=wb_grouped[:, q, half].rearrange("p c k -> p (c k)"),
+                )
+            kv_ps = products.tile([P, QUARTER_ROWS], F32, tag="product")
+            nc.tensor.matmul_mx(
+                out=kv_ps[:],
+                lhsT=cn_codes[:].bitcast(FP8X4),
+                lhsT_scale=cn_scales[:],
+                rhs=wb_codes[:, q, :].bitcast(FP8X4),
+                rhs_scale=wb_scales[:, q, :],
+                start=True,
+                stop=True,
+            )
+            kv_cols = slice(QUARTER_ROWS * q, QUARTER_ROWS * (q + 1))
+            copy_out = nc.scalar.copy if q % 2 == 0 else nc.vector.tensor_copy
+            copy_out(
+                out=kv_sb[:, kv_cols].rearrange("p (n i) -> p n i", i=PACK),
+                in_=kv_ps[:].rearrange("p (i n) -> p n i", i=PACK),
+            )
+            heads = slice(HEADS_PER_QUARTER * q, HEADS_PER_QUARTER * (q + 1))
+            for b in range(BATCH):
+                by_head = kv_sb[SEQ * b : SEQ * (b + 1), kv_cols].rearrange(
+                    "s (h c) -> s h c", c=HEAD_COLS
+                )
+                nc.sync.dma_start(
+                    out=key_s[b, heads, :, 0:HALF_HEAD].rearrange("h s d -> s h d"),
+                    in_=by_head[:, :, 0:HALF_HEAD],
+                )
+                nc.sync.dma_start(
+                    out=v[b, heads].rearrange("h s d -> s h d"),
+                    in_=by_head[:, :, HALF_HEAD:HEAD_COLS],
+                )

@@ -8,6 +8,7 @@ F32 = mybir.dt.float32
 BF16 = mybir.dt.bfloat16
 U32 = mybir.dt.uint32
 U8 = mybir.dt.uint8
+I32 = mybir.dt.int32
 FP8X4 = mybir.dt.float8_e4m3fn_x4
 ACT = mybir.ActivationFunctionType
 ALU = mybir.AluOpType
@@ -59,7 +60,8 @@ def tile_modelnew_pb_s_kernel(
         for q in range(QUARTERS):
             nc.sync.dma_start(out=wb_sb[:, q], in_=wb_rows[q])
         pe_sb = keep.tile([P, ROPE], BF16)
-        nc.scalar.dma_start(out=pe_sb[:], in_=k_pe_raw.flatten_outer_dims())
+        for b in range(BATCH):
+            nc.scalar.dma_start(out=pe_sb[b:P:BATCH, :], in_=k_pe_raw[b])
         gain_bf = keep.tile([P, 2, 2], BF16)
         nc.scalar.dma_start(out=gain_bf[:], in_=kv_a_ln_w.rearrange("(u p e) -> p u e", u=2, e=2))
 
@@ -67,15 +69,14 @@ def tile_modelnew_pb_s_kernel(
         make_identity(nc, ident[:])
         ones = keep.tile([P, P], F32)
         nc.gpsimd.memset(ones[:], 1.0)
+        partition_no = keep.tile([P, 1], I32)
+        nc.gpsimd.iota(partition_no[:], pattern=[[0, 1]], base=0, channel_multiplier=1)
+        pos_int = keep.tile([P, 1], I32)
+        nc.vector.tensor_single_scalar(
+            out=pos_int[:], in_=partition_no[:], scalar=1, op=ALU.arith_shift_right
+        )
         pos = keep.tile([P, 1], F32)
-        for b in range(BATCH):
-            nc.gpsimd.iota(
-                pos[SEQ * b : SEQ * (b + 1), :],
-                pattern=[[0, 1]],
-                base=0,
-                channel_multiplier=1,
-                allow_small_or_imprecise_dtypes=True,
-            )
+        nc.vector.tensor_copy(out=pos[:], in_=pos_int[:])
 
         freq = keep.tile([P, 2, ROPE_HALF], F32)
         nc.vector.memset(freq[:, :, 0:1], 1.0)
@@ -139,9 +140,11 @@ def tile_modelnew_pb_s_kernel(
         for g in range(PASSES_1):
             transpose_words(nc, x_bank[:, g], x_sb[:, KR * g : KR * (g + 1)], ident[:])
         x_grouped = keep.tile([P, PASSES_1, TOK, PACK], BF16, align_bytes=64)
-        nc.vector.tensor_copy(
-            out=x_grouped[:].bitcast(F32), in_=x_bank[:].rearrange("p g u r -> p g r u")
-        )
+        for g in range(PASSES_1):
+            nc.vector.tensor_copy(
+                out=x_grouped[:, g].bitcast(F32).rearrange("p (s b) u -> p s b u", b=BATCH),
+                in_=x_bank[:, g].rearrange("p u (b s) -> p s b u", b=BATCH),
+            )
         x_codes = keep.tile([P, PASSES_1, TOK], U32, align_bytes=64)
         x_scales = keep.tile([P, PASSES_1, TOK], U8, align_bytes=64)
         nc.vector.quantize_mx(
@@ -214,7 +217,7 @@ def tile_modelnew_pb_s_kernel(
         for b in range(BATCH):
             nc.sync.dma_start(
                 out=key_s[b].rearrange("h s d -> s h d")[:, :, HALF_HEAD:HEAD_COLS],
-                in_=rope[SEQ * b : SEQ * (b + 1), :].unsqueeze(1).to_broadcast([SEQ, HEADS, ROPE]),
+                in_=rope[b:P:BATCH, :].unsqueeze(1).to_broadcast([SEQ, HEADS, ROPE]),
             )
 
         wb_grouped = keep.tile([P, QUARTERS, 2, 2 * P, PACK], BF16, align_bytes=64)
@@ -255,9 +258,7 @@ def tile_modelnew_pb_s_kernel(
             )
             heads = slice(HEADS_PER_QUARTER * q, HEADS_PER_QUARTER * (q + 1))
             for b in range(BATCH):
-                by_head = kv_sb[SEQ * b : SEQ * (b + 1), kv_cols].rearrange(
-                    "s (h c) -> s h c", c=HEAD_COLS
-                )
+                by_head = kv_sb[b:P:BATCH, kv_cols].rearrange("s (h c) -> s h c", c=HEAD_COLS)
                 nc.sync.dma_start(
                     out=key_s[b, heads, :, 0:HALF_HEAD].rearrange("h s d -> s h d"),
                     in_=by_head[:, :, 0:HALF_HEAD],

@@ -48,6 +48,7 @@ def tile_modelnew_pb_s_kernel(
         staging = ctx.enter_context(tc.psum_pool(name="staging", bufs=3))
         products = ctx.enter_context(tc.psum_pool(name="products", bufs=4))
         norm_psum = ctx.enter_context(tc.psum_pool(name="norm_psum", bufs=1))
+        ctx.enter_context(tc.manual_schedule())
 
         x_sb = keep.tile([P, D], BF16)
         nc.sync.dma_start(out=x_sb[:], in_=hidden_states.flatten_outer_dims())
@@ -65,18 +66,12 @@ def tile_modelnew_pb_s_kernel(
         gain_bf = keep.tile([P, 2, 2], BF16)
         nc.scalar.dma_start(out=gain_bf[:], in_=kv_a_ln_w.rearrange("(u p e) -> p u e", u=2, e=2))
 
+        partition_no = keep.tile([P, 1], I32)
+        nc.gpsimd.iota(partition_no[:], pattern=[[0, 1]], base=0, channel_multiplier=1)
         ident = keep.tile([P, P], F32)
         make_identity(nc, ident[:])
         ones = keep.tile([P, P], F32)
-        nc.gpsimd.memset(ones[:], 1.0)
-        partition_no = keep.tile([P, 1], I32)
-        nc.gpsimd.iota(partition_no[:], pattern=[[0, 1]], base=0, channel_multiplier=1)
-        pos_int = keep.tile([P, 1], I32)
-        nc.vector.tensor_single_scalar(
-            out=pos_int[:], in_=partition_no[:], scalar=1, op=ALU.arith_shift_right
-        )
-        pos = keep.tile([P, 1], F32)
-        nc.vector.tensor_copy(out=pos[:], in_=pos_int[:])
+        nc.vector.memset(ones[:], 1.0)
 
         freq = keep.tile([P, 2, ROPE_HALF], F32)
         nc.vector.memset(freq[:, :, 0:1], 1.0)
@@ -93,6 +88,12 @@ def tile_modelnew_pb_s_kernel(
         nc.vector.tensor_scalar(
             out=eps[:], in0=freq[:, 0, 0:1], scalar1=EPS, scalar2=None, op0=ALU.mult
         )
+        pos_int = keep.tile([P, 1], I32)
+        nc.vector.tensor_single_scalar(
+            out=pos_int[:], in_=partition_no[:], scalar=1, op=ALU.arith_shift_right
+        )
+        pos = keep.tile([P, 1], F32)
+        nc.vector.tensor_copy(out=pos[:], in_=pos_int[:])
         turns = keep.tile([P, 2, ROPE_HALF], F32)
         nc.vector.tensor_scalar(
             out=turns[:],
@@ -119,6 +120,8 @@ def tile_modelnew_pb_s_kernel(
         table_warm = keep.tile([P, 1], F32)
         nc.scalar.activation(out=table_warm[:], in_=sin_cos[:, 1, 0:1], func=ACT.Abs_reciprocal_sqrt)
 
+        gain = keep.tile([P, CHUNKS], F32)
+        nc.gpsimd.tensor_copy(out=gain[:], in_=gain_bf[:].rearrange("p u e -> p (u e)"))
         prod = keep.tile([P, 2, 2, ROPE_HALF], F32)
         nc.gpsimd.tensor_tensor(
             out=prod[:],
@@ -133,45 +136,73 @@ def tile_modelnew_pb_s_kernel(
         nc.gpsimd.tensor_tensor(
             out=rope[:, ROPE_HALF:ROPE], in0=prod[:, 1, 1, :], in1=prod[:, 0, 0, :], op=ALU.add
         )
-        gain = keep.tile([P, CHUNKS], F32)
-        nc.gpsimd.tensor_copy(out=gain[:], in_=gain_bf[:].rearrange("p u e -> p (u e)"))
+        for b in range(BATCH):
+            nc.sync.dma_start(
+                out=key_s[b].rearrange("h s d -> s h d")[:, :, HALF_HEAD:HEAD_COLS],
+                in_=rope[b:P:BATCH, :].unsqueeze(1).to_broadcast([SEQ, HEADS, ROPE]),
+            )
 
+        x_grouped = keep.tile([P, PASSES_1, TOK, PACK], BF16, align_bytes=64)
+        x_codes = keep.tile([P, PASSES_1, TOK], U32, align_bytes=64)
+        x_scales = keep.tile([P, PASSES_1, TOK], U8, align_bytes=64)
         x_bank = staging.tile([P, PASSES_1, 2, TOK], F32, tag="bank")
         for g in range(PASSES_1):
             transpose_words(nc, x_bank[:, g], x_sb[:, KR * g : KR * (g + 1)], ident[:])
-        x_grouped = keep.tile([P, PASSES_1, TOK, PACK], BF16, align_bytes=64)
         for g in range(PASSES_1):
             nc.vector.tensor_copy(
                 out=x_grouped[:, g].bitcast(F32).rearrange("p (s b) u -> p s b u", b=BATCH),
                 in_=x_bank[:, g].rearrange("p u (b s) -> p s b u", b=BATCH),
             )
-        x_codes = keep.tile([P, PASSES_1, TOK], U32, align_bytes=64)
-        x_scales = keep.tile([P, PASSES_1, TOK], U8, align_bytes=64)
-        nc.vector.quantize_mx(
-            out=x_codes[:].rearrange("p g r -> p (g r)").bitcast(FP8X4),
-            scales=x_scales[:].rearrange("p g r -> p (g r)"),
-            in_=x_grouped[:].rearrange("p g r k -> p (g r k)"),
-        )
 
         wa_grouped = keep.tile([P, CHUNKS, PASSES_1, P, PACK], BF16, align_bytes=64)
         wa_codes = keep.tile([P, CHUNKS, PASSES_1, P], U32, align_bytes=64)
         wa_scales = keep.tile([P, CHUNKS, PASSES_1, P], U8, align_bytes=64)
-        squares = keep.tile([P, CHUNKS, TOK], F32)
-        gained = keep.tile([P, CHUNKS, TOK], F32)
-        sum_sq = norm_psum.tile([P, TOK], F32)
         for t in range(CHUNKS):
             wa_bank = staging.tile([P, PASSES_1, 2, P], F32, tag="bank")
             for g in range(PASSES_1):
                 transpose_words(nc, wa_bank[:, g], wa_sb[:, t, KR * g : KR * (g + 1)], ident[:])
-            copy_out = nc.scalar.copy if t % 2 == 0 else nc.vector.tensor_copy
+            copy_out = nc.vector.tensor_copy if t == 0 else nc.scalar.copy
             copy_out(
                 out=wa_grouped[:, t].bitcast(F32), in_=wa_bank[:].rearrange("p g u m -> p g m u")
             )
+            if t == 0:
+                nc.vector.quantize_mx(
+                    out=x_codes[:].rearrange("p g r -> p (g r)").bitcast(FP8X4),
+                    scales=x_scales[:].rearrange("p g r -> p (g r)"),
+                    in_=x_grouped[:].rearrange("p g r k -> p (g r k)"),
+                )
             nc.vector.quantize_mx(
                 out=wa_codes[:, t].rearrange("p g m -> p (g m)").bitcast(FP8X4),
                 scales=wa_scales[:, t].rearrange("p g m -> p (g m)"),
                 in_=wa_grouped[:, t].rearrange("p g m k -> p (g m k)"),
             )
+
+        wb_grouped = keep.tile([P, QUARTERS, 2, 2 * P, PACK], BF16, align_bytes=64)
+        wb_codes = keep.tile([P, QUARTERS, QUARTER_ROWS], U32, align_bytes=64)
+        wb_scales = keep.tile([P, QUARTERS, QUARTER_ROWS], U8, align_bytes=64)
+
+        def transpose_and_regroup_wb(q, half):
+            wb_bank = staging.tile([P, 2, 2, P], F32, tag="bank")
+            for j in range(2):
+                transpose_words(nc, wb_bank[:, j], wb_sb[:, q, 2 * half + j, :], ident[:])
+            copy_out = nc.vector.tensor_copy if q == 0 else nc.scalar.copy
+            copy_out(
+                out=wb_grouped[:, q, half].bitcast(F32).rearrange("p (j n) u -> p j n u", j=2),
+                in_=wb_bank[:].rearrange("p j u n -> p j n u"),
+            )
+
+        def quantise_wb(q, half):
+            cols = slice(2 * P * half, 2 * P * (half + 1))
+            nc.vector.quantize_mx(
+                out=wb_codes[:, q, cols].bitcast(FP8X4),
+                scales=wb_scales[:, q, cols],
+                in_=wb_grouped[:, q, half].rearrange("p c k -> p (c k)"),
+            )
+
+        squares = keep.tile([P, CHUNKS, TOK], F32)
+        gained = keep.tile([P, CHUNKS, TOK], F32)
+
+        def first_product(t):
             ckv_t = products.tile([P, TOK], F32, tag="product")
             for g in range(PASSES_1):
                 nc.tensor.matmul_mx(
@@ -184,21 +215,37 @@ def tile_modelnew_pb_s_kernel(
                     stop=(g == PASSES_1 - 1),
                 )
             nc.scalar.activation(out=squares[:, t, :], in_=ckv_t[:], func=ACT.Square)
-            nc.scalar.activation(
-                out=gained[:, t, :], in_=ckv_t[:], func=ACT.Copy, scale=gain[:, t : t + 1]
-            )
-            nc.tensor.matmul(
-                out=sum_sq[:],
-                lhsT=ones[:],
-                rhs=squares[:, t, :],
-                start=(t == 0),
-                stop=(t == CHUNKS - 1),
+            nc.vector.tensor_scalar(
+                out=gained[:, t, :], in0=ckv_t[:], scalar1=gain[:, t : t + 1], scalar2=None, op0=ALU.mult
             )
 
+        first_product(0)
+        first_product(1)
+        squares_01 = keep.tile([P, TOK], F32)
+        nc.vector.tensor_tensor(
+            out=squares_01[:], in0=squares[:, 0, :], in1=squares[:, 1, :], op=ALU.add
+        )
+        first_product(2)
+        squares_012 = keep.tile([P, TOK], F32)
+        nc.vector.tensor_tensor(
+            out=squares_012[:], in0=squares_01[:], in1=squares[:, 2, :], op=ALU.add
+        )
+        transpose_and_regroup_wb(0, 0)
+        first_product(CHUNKS - 1)
+        quantise_wb(0, 0)
+        transpose_and_regroup_wb(0, 1)
+
+        sum_sq = norm_psum.tile([P, TOK], F32)
+        nc.tensor.matmul(out=sum_sq[:], lhsT=ones[:], rhs=squares_012[:], start=True, stop=False)
+        nc.tensor.matmul(
+            out=sum_sq[:], lhsT=ones[:], rhs=squares[:, CHUNKS - 1, :], start=False, stop=True
+        )
         rstd = keep.tile([P, TOK], F32)
         nc.scalar.activation(
             out=rstd[:], in_=sum_sq[:], func=ACT.Abs_reciprocal_sqrt, bias=eps[:, 0:1], scale=1.0 / KR
         )
+        quantise_wb(0, 1)
+        transpose_and_regroup_wb(1, 0)
         cn_grouped = keep.tile([P, TOK, PACK], BF16, align_bytes=64)
         nc.vector.tensor_tensor(
             out=cn_grouped[:],
@@ -213,33 +260,11 @@ def tile_modelnew_pb_s_kernel(
             scales=cn_scales[:],
             in_=cn_grouped[:].rearrange("p r k -> p (r k)"),
         )
+        quantise_wb(1, 0)
 
-        for b in range(BATCH):
-            nc.sync.dma_start(
-                out=key_s[b].rearrange("h s d -> s h d")[:, :, HALF_HEAD:HEAD_COLS],
-                in_=rope[b:P:BATCH, :].unsqueeze(1).to_broadcast([SEQ, HEADS, ROPE]),
-            )
-
-        wb_grouped = keep.tile([P, QUARTERS, 2, 2 * P, PACK], BF16, align_bytes=64)
-        wb_codes = keep.tile([P, QUARTERS, QUARTER_ROWS], U32, align_bytes=64)
-        wb_scales = keep.tile([P, QUARTERS, QUARTER_ROWS], U8, align_bytes=64)
         kv_sb = keep.tile([P, HEADS * HEAD_COLS], F32)
-        for q in range(QUARTERS):
-            for half in range(2):
-                wb_bank = staging.tile([P, 2, 2, P], F32, tag="bank")
-                for j in range(2):
-                    transpose_words(nc, wb_bank[:, j], wb_sb[:, q, 2 * half + j, :], ident[:])
-                copy_out = nc.scalar.copy if half == 0 else nc.vector.tensor_copy
-                copy_out(
-                    out=wb_grouped[:, q, half].bitcast(F32).rearrange("p (j n) u -> p j n u", j=2),
-                    in_=wb_bank[:].rearrange("p j u n -> p j n u"),
-                )
-                cols = slice(2 * P * half, 2 * P * (half + 1))
-                nc.vector.quantize_mx(
-                    out=wb_codes[:, q, cols].bitcast(FP8X4),
-                    scales=wb_scales[:, q, cols],
-                    in_=wb_grouped[:, q, half].rearrange("p c k -> p (c k)"),
-                )
+
+        def second_product(q):
             kv_ps = products.tile([P, QUARTER_ROWS], F32, tag="product")
             nc.tensor.matmul_mx(
                 out=kv_ps[:],
@@ -251,8 +276,7 @@ def tile_modelnew_pb_s_kernel(
                 stop=True,
             )
             kv_cols = slice(QUARTER_ROWS * q, QUARTER_ROWS * (q + 1))
-            copy_out = nc.scalar.copy if q % 2 == 0 else nc.vector.tensor_copy
-            copy_out(
+            nc.vector.tensor_copy(
                 out=kv_sb[:, kv_cols].rearrange("p (n i) -> p n i", i=PACK),
                 in_=kv_ps[:].rearrange("p (i n) -> p n i", i=PACK),
             )
@@ -267,3 +291,15 @@ def tile_modelnew_pb_s_kernel(
                     out=v[b, heads].rearrange("h s d -> s h d"),
                     in_=by_head[:, :, HALF_HEAD:HEAD_COLS],
                 )
+
+        transpose_and_regroup_wb(1, 1)
+        quantise_wb(1, 1)
+        for half in range(2):
+            transpose_and_regroup_wb(2, half)
+            quantise_wb(2, half)
+        second_product(0)
+        for half in range(2):
+            transpose_and_regroup_wb(3, half)
+            quantise_wb(3, half)
+            second_product(1 + half)
+        second_product(3)

@@ -28,6 +28,7 @@ QUARTER_ROWS = HEADS * HEAD_COLS // QUARTERS
 HEADS_PER_QUARTER = HEADS // QUARTERS
 EPS = 1e-6
 THETA = 10000.0
+WARM_BEFORE_LOADS = 4
 ROUND_MAGIC = 12582912.0
 
 FLOPS = 2 * TOK * D * KR + 2 * TOK * KR * HEADS * HEAD_COLS
@@ -72,6 +73,14 @@ def tile_modelnew_pb_s_kernel(
         make_identity(nc, ident[:])
         ones = keep.tile([P, P], F32)
         nc.vector.memset(ones[:], 1.0)
+
+        idle_ps = norm_psum.tile([P, P], F32, tag="norm")
+
+        def keep_clock_up():
+            nc.tensor.matmul(out=idle_ps[:], lhsT=ones[:], rhs=ones[:], start=True, stop=True)
+
+        for i in range(WARM_BEFORE_LOADS):
+            keep_clock_up()
 
         freq = keep.tile([P, 2, ROPE_HALF], F32)
         nc.vector.memset(freq[:, :, 0:1], 1.0)
@@ -148,6 +157,7 @@ def tile_modelnew_pb_s_kernel(
         x_bank = staging.tile([P, PASSES_1, 2, TOK], F32, tag="bank")
         for g in range(PASSES_1):
             transpose_words(nc, x_bank[:, g], x_sb[:, KR * g : KR * (g + 1)], ident[:])
+        keep_clock_up()
         for g in range(PASSES_1):
             nc.vector.tensor_copy(
                 out=x_grouped[:, g].bitcast(F32).rearrange("p (s b) u -> p s b u", b=BATCH),
@@ -161,6 +171,8 @@ def tile_modelnew_pb_s_kernel(
             wa_bank = staging.tile([P, PASSES_1, 2, P], F32, tag="bank")
             for g in range(PASSES_1):
                 transpose_words(nc, wa_bank[:, g], wa_sb[:, t, KR * g : KR * (g + 1)], ident[:])
+            if t < CHUNKS - 2:
+                keep_clock_up()
             copy_out = nc.vector.tensor_copy if t == 0 else nc.scalar.copy
             copy_out(
                 out=wa_grouped[:, t].bitcast(F32), in_=wa_bank[:].rearrange("p g u m -> p g m u")
@@ -235,7 +247,7 @@ def tile_modelnew_pb_s_kernel(
         quantise_wb(0, 0)
         transpose_and_regroup_wb(0, 1)
 
-        sum_sq = norm_psum.tile([P, TOK], F32)
+        sum_sq = norm_psum.tile([P, TOK], F32, tag="norm")
         nc.tensor.matmul(out=sum_sq[:], lhsT=ones[:], rhs=squares_012[:], start=True, stop=False)
         nc.tensor.matmul(
             out=sum_sq[:], lhsT=ones[:], rhs=squares[:, CHUNKS - 1, :], start=False, stop=True

@@ -15,20 +15,22 @@ ALU = mybir.AluOpType
 
 P = 128
 PACK = 4
+K_PASS = P * PACK
 BATCH, SEQ = 2, 64
 TOK = BATCH * SEQ
 D = 1024
 KR = 512
 HEADS, HEAD_COLS, HALF_HEAD = 16, 128, 64
 ROPE, ROPE_HALF = 64, 32
-PASSES_1 = D // (P * PACK)
+PASSES_1 = D // K_PASS
 CHUNKS = KR // P
 QUARTERS = 4
-QUARTER_ROWS = HEADS * HEAD_COLS // QUARTERS
+QUARTER_COLS = HEADS * HEAD_COLS // QUARTERS
 HEADS_PER_QUARTER = HEADS // QUARTERS
+WB_BANKS = 2 * QUARTERS
+BANK_ROWS = QUARTER_COLS // 2
 EPS = 1e-6
 THETA = 10000.0
-WARM_BEFORE_LOADS = 4
 ROUND_MAGIC = 12582912.0
 
 FLOPS = 2 * TOK * D * KR + 2 * TOK * KR * HEADS * HEAD_COLS
@@ -38,6 +40,10 @@ def transpose_words(nc, bank, rows_bf16, ident):
     words = rows_bf16.bitcast(F32)
     for u in range(2):
         nc.tensor.transpose(bank[:, u, :], words[:, P * u : P * (u + 1)], ident)
+
+
+def quantise(nc, codes, scales, grouped):
+    nc.vector.quantize_mx(out=codes.bitcast(FP8X4), scales=scales, in_=grouped)
 
 
 def tile_modelnew_pb_s_kernel(
@@ -57,30 +63,22 @@ def tile_modelnew_pb_s_kernel(
         wa_rows = kv_a_w_ckv.rearrange("(u p e) k -> u e p k", u=2, e=2)
         for t in range(CHUNKS):
             nc.sync.dma_start(out=wa_sb[:, t, :], in_=wa_rows[t // 2, t % 2])
-        wb_sb = keep.tile([P, QUARTERS, PACK, KR], BF16)
-        wb_rows = kv_b_w.rearrange("(q p i) k -> q p i k", q=QUARTERS, i=PACK)
-        for q in range(QUARTERS):
-            nc.sync.dma_start(out=wb_sb[:, q], in_=wb_rows[q])
+        gain_bf = keep.tile([P, 2, 2], BF16)
+        nc.sync.dma_start(out=gain_bf[:], in_=kv_a_ln_w.rearrange("(u p e) -> p u e", u=2, e=2))
         pe_sb = keep.tile([P, ROPE], BF16)
         for b in range(BATCH):
-            nc.scalar.dma_start(out=pe_sb[b:P:BATCH, :], in_=k_pe_raw[b])
-        gain_bf = keep.tile([P, 2, 2], BF16)
-        nc.scalar.dma_start(out=gain_bf[:], in_=kv_a_ln_w.rearrange("(u p e) -> p u e", u=2, e=2))
+            nc.sync.dma_start(out=pe_sb[b:P:BATCH, :], in_=k_pe_raw[b])
+        wb_sb = keep.tile([P, QUARTERS, PACK, KR], BF16)
+        wb_rows = kv_b_w.rearrange("(q n i) k -> q n i k", q=QUARTERS, i=PACK)
+        for q in range(QUARTERS):
+            nc.sync.dma_start(out=wb_sb[:, q], in_=wb_rows[q])
 
         partition_no = keep.tile([P, 1], I32)
         nc.gpsimd.iota(partition_no[:], pattern=[[0, 1]], base=0, channel_multiplier=1)
         ident = keep.tile([P, P], F32)
         make_identity(nc, ident[:])
         ones = keep.tile([P, P], F32)
-        nc.vector.memset(ones[:], 1.0)
-
-        idle_ps = norm_psum.tile([P, P], F32, tag="norm")
-
-        def keep_clock_up():
-            nc.tensor.matmul(out=idle_ps[:], lhsT=ones[:], rhs=ones[:], start=True, stop=True)
-
-        for i in range(WARM_BEFORE_LOADS):
-            keep_clock_up()
+        nc.gpsimd.memset(ones[:], 1.0)
 
         freq = keep.tile([P, 2, ROPE_HALF], F32)
         nc.vector.memset(freq[:, :, 0:1], 1.0)
@@ -156,8 +154,7 @@ def tile_modelnew_pb_s_kernel(
         x_scales = keep.tile([P, PASSES_1, TOK], U8, align_bytes=64)
         x_bank = staging.tile([P, PASSES_1, 2, TOK], F32, tag="bank")
         for g in range(PASSES_1):
-            transpose_words(nc, x_bank[:, g], x_sb[:, KR * g : KR * (g + 1)], ident[:])
-        keep_clock_up()
+            transpose_words(nc, x_bank[:, g], x_sb[:, K_PASS * g : K_PASS * (g + 1)], ident[:])
         for g in range(PASSES_1):
             nc.vector.tensor_copy(
                 out=x_grouped[:, g].bitcast(F32).rearrange("p (s b) u -> p s b u", b=BATCH),
@@ -170,45 +167,48 @@ def tile_modelnew_pb_s_kernel(
         for t in range(CHUNKS):
             wa_bank = staging.tile([P, PASSES_1, 2, P], F32, tag="bank")
             for g in range(PASSES_1):
-                transpose_words(nc, wa_bank[:, g], wa_sb[:, t, KR * g : KR * (g + 1)], ident[:])
-            if t < CHUNKS - 2:
-                keep_clock_up()
+                transpose_words(
+                    nc, wa_bank[:, g], wa_sb[:, t, K_PASS * g : K_PASS * (g + 1)], ident[:]
+                )
             copy_out = nc.vector.tensor_copy if t == 0 else nc.scalar.copy
             copy_out(
                 out=wa_grouped[:, t].bitcast(F32), in_=wa_bank[:].rearrange("p g u m -> p g m u")
             )
             if t == 0:
-                nc.vector.quantize_mx(
-                    out=x_codes[:].rearrange("p g r -> p (g r)").bitcast(FP8X4),
-                    scales=x_scales[:].rearrange("p g r -> p (g r)"),
-                    in_=x_grouped[:].rearrange("p g r k -> p (g r k)"),
+                quantise(
+                    nc,
+                    x_codes[:].rearrange("p g r -> p (g r)"),
+                    x_scales[:].rearrange("p g r -> p (g r)"),
+                    x_grouped[:].rearrange("p g r k -> p (g r k)"),
                 )
-            nc.vector.quantize_mx(
-                out=wa_codes[:, t].rearrange("p g m -> p (g m)").bitcast(FP8X4),
-                scales=wa_scales[:, t].rearrange("p g m -> p (g m)"),
-                in_=wa_grouped[:, t].rearrange("p g m k -> p (g m k)"),
+            quantise(
+                nc,
+                wa_codes[:, t].rearrange("p g m -> p (g m)"),
+                wa_scales[:, t].rearrange("p g m -> p (g m)"),
+                wa_grouped[:, t].rearrange("p g m k -> p (g m k)"),
             )
 
-        wb_grouped = keep.tile([P, QUARTERS, 2, 2 * P, PACK], BF16, align_bytes=64)
-        wb_codes = keep.tile([P, QUARTERS, QUARTER_ROWS], U32, align_bytes=64)
-        wb_scales = keep.tile([P, QUARTERS, QUARTER_ROWS], U8, align_bytes=64)
+        wb_grouped = keep.tile([P, WB_BANKS, BANK_ROWS, PACK], BF16, align_bytes=64)
+        wb_codes = keep.tile([P, WB_BANKS, BANK_ROWS], U32, align_bytes=64)
+        wb_scales = keep.tile([P, WB_BANKS, BANK_ROWS], U8, align_bytes=64)
 
-        def transpose_and_regroup_wb(q, half):
+        def transpose_and_regroup_wb(bank_no):
             wb_bank = staging.tile([P, 2, 2, P], F32, tag="bank")
             for j in range(2):
-                transpose_words(nc, wb_bank[:, j], wb_sb[:, q, 2 * half + j, :], ident[:])
-            copy_out = nc.vector.tensor_copy if q == 0 else nc.scalar.copy
+                rows = wb_sb[:, bank_no // 2, 2 * (bank_no % 2) + j, :]
+                transpose_words(nc, wb_bank[:, j], rows, ident[:])
+            copy_out = nc.vector.tensor_copy if bank_no == 0 else nc.scalar.copy
             copy_out(
-                out=wb_grouped[:, q, half].bitcast(F32).rearrange("p (j n) u -> p j n u", j=2),
+                out=wb_grouped[:, bank_no].bitcast(F32).rearrange("p (j n) u -> p j n u", j=2),
                 in_=wb_bank[:].rearrange("p j u n -> p j n u"),
             )
 
-        def quantise_wb(q, half):
-            cols = slice(2 * P * half, 2 * P * (half + 1))
-            nc.vector.quantize_mx(
-                out=wb_codes[:, q, cols].bitcast(FP8X4),
-                scales=wb_scales[:, q, cols],
-                in_=wb_grouped[:, q, half].rearrange("p c k -> p (c k)"),
+        def quantise_wb(bank_no):
+            quantise(
+                nc,
+                wb_codes[:, bank_no, :],
+                wb_scales[:, bank_no, :],
+                wb_grouped[:, bank_no].rearrange("p c k -> p (c k)"),
             )
 
         squares = keep.tile([P, CHUNKS, TOK], F32)
@@ -242,22 +242,20 @@ def tile_modelnew_pb_s_kernel(
         nc.vector.tensor_tensor(
             out=squares_012[:], in0=squares_01[:], in1=squares[:, 2, :], op=ALU.add
         )
-        transpose_and_regroup_wb(0, 0)
-        first_product(CHUNKS - 1)
-        quantise_wb(0, 0)
-        transpose_and_regroup_wb(0, 1)
+        transpose_and_regroup_wb(0)
+        first_product(3)
+        quantise_wb(0)
+        transpose_and_regroup_wb(1)
 
-        sum_sq = norm_psum.tile([P, TOK], F32, tag="norm")
+        sum_sq = norm_psum.tile([P, TOK], F32)
         nc.tensor.matmul(out=sum_sq[:], lhsT=ones[:], rhs=squares_012[:], start=True, stop=False)
-        nc.tensor.matmul(
-            out=sum_sq[:], lhsT=ones[:], rhs=squares[:, CHUNKS - 1, :], start=False, stop=True
-        )
+        nc.tensor.matmul(out=sum_sq[:], lhsT=ones[:], rhs=squares[:, 3, :], start=False, stop=True)
         rstd = keep.tile([P, TOK], F32)
         nc.scalar.activation(
             out=rstd[:], in_=sum_sq[:], func=ACT.Abs_reciprocal_sqrt, bias=eps[:, 0:1], scale=1.0 / KR
         )
-        quantise_wb(0, 1)
-        transpose_and_regroup_wb(1, 0)
+        quantise_wb(1)
+        transpose_and_regroup_wb(2)
         cn_grouped = keep.tile([P, TOK, PACK], BF16, align_bytes=64)
         nc.vector.tensor_tensor(
             out=cn_grouped[:],
@@ -267,28 +265,25 @@ def tile_modelnew_pb_s_kernel(
         )
         cn_codes = keep.tile([P, TOK], U32, align_bytes=64)
         cn_scales = keep.tile([P, TOK], U8, align_bytes=64)
-        nc.vector.quantize_mx(
-            out=cn_codes[:].bitcast(FP8X4),
-            scales=cn_scales[:],
-            in_=cn_grouped[:].rearrange("p r k -> p (r k)"),
-        )
-        quantise_wb(1, 0)
+        quantise(nc, cn_codes[:], cn_scales[:], cn_grouped[:].rearrange("p r k -> p (r k)"))
+        quantise_wb(2)
 
         kv_sb = keep.tile([P, HEADS * HEAD_COLS], F32)
 
         def second_product(q):
-            kv_ps = products.tile([P, QUARTER_ROWS], F32, tag="product")
+            kv_ps = products.tile([P, QUARTER_COLS], F32, tag="product")
             nc.tensor.matmul_mx(
                 out=kv_ps[:],
                 lhsT=cn_codes[:].bitcast(FP8X4),
                 lhsT_scale=cn_scales[:],
-                rhs=wb_codes[:, q, :].bitcast(FP8X4),
-                rhs_scale=wb_scales[:, q, :],
+                rhs=wb_codes[:, 2 * q : 2 * q + 2, :].rearrange("p h c -> p (h c)").bitcast(FP8X4),
+                rhs_scale=wb_scales[:, 2 * q : 2 * q + 2, :].rearrange("p h c -> p (h c)"),
                 start=True,
                 stop=True,
             )
-            kv_cols = slice(QUARTER_ROWS * q, QUARTER_ROWS * (q + 1))
-            nc.vector.tensor_copy(
+            kv_cols = slice(QUARTER_COLS * q, QUARTER_COLS * (q + 1))
+            copy_out = nc.scalar.copy if q == 2 else nc.vector.tensor_copy
+            copy_out(
                 out=kv_sb[:, kv_cols].rearrange("p (n i) -> p n i", i=PACK),
                 in_=kv_ps[:].rearrange("p (i n) -> p n i", i=PACK),
             )
@@ -304,14 +299,9 @@ def tile_modelnew_pb_s_kernel(
                     in_=by_head[:, :, HALF_HEAD:HEAD_COLS],
                 )
 
-        transpose_and_regroup_wb(1, 1)
-        quantise_wb(1, 1)
-        for half in range(2):
-            transpose_and_regroup_wb(2, half)
-            quantise_wb(2, half)
-        second_product(0)
-        for half in range(2):
-            transpose_and_regroup_wb(3, half)
-            quantise_wb(3, half)
-            second_product(1 + half)
-        second_product(3)
+        for bank_no in range(3, WB_BANKS):
+            transpose_and_regroup_wb(bank_no)
+            if bank_no >= WB_BANKS - 3:
+                second_product(bank_no - (WB_BANKS - 3))
+            quantise_wb(bank_no)
+        second_product(QUARTERS - 1)

import math
from contextlib import ExitStack

import concourse.mybir as mybir
from concourse.masks import make_identity

F32 = mybir.dt.float32
BF16 = mybir.dt.bfloat16
U32 = mybir.dt.uint32
U8 = mybir.dt.uint8
I32 = mybir.dt.int32
FP8X4 = mybir.dt.float8_e4m3fn_x4
ACT = mybir.ActivationFunctionType
ALU = mybir.AluOpType

P = 128
PACK = 4
K_PASS = P * PACK
BATCH, SEQ = 2, 64
TOK = BATCH * SEQ
D = 1024
KR = 512
HEADS, HEAD_COLS, HALF_HEAD = 16, 128, 64
ROPE, ROPE_HALF = 64, 32
PASSES_1 = D // K_PASS
CHUNKS = KR // P
QUARTERS = 4
QUARTER_COLS = HEADS * HEAD_COLS // QUARTERS
HEADS_PER_QUARTER = HEADS // QUARTERS
WB_BANKS = 2 * QUARTERS
BANK_ROWS = QUARTER_COLS // 2
EPS = 1e-6
THETA = 10000.0
ROUND_MAGIC = 12582912.0

FLOPS = 2 * TOK * D * KR + 2 * TOK * KR * HEADS * HEAD_COLS


def transpose_words(nc, bank, rows_bf16, ident):
    words = rows_bf16.bitcast(F32)
    for u in range(2):
        nc.tensor.transpose(bank[:, u, :], words[:, P * u : P * (u + 1)], ident)


def quantise(nc, codes, scales, grouped):
    nc.vector.quantize_mx(out=codes.bitcast(FP8X4), scales=scales, in_=grouped)


def tile_modelnew_pb_s_kernel(
    tc, hidden_states, kv_a_w_ckv, k_pe_raw, kv_a_ln_w, kv_b_w, key_s, v
):
    nc = tc.nc
    with ExitStack() as ctx:
        keep = ctx.enter_context(tc.tile_pool(name="keep", bufs=1))
        staging = ctx.enter_context(tc.psum_pool(name="staging", bufs=3))
        products = ctx.enter_context(tc.psum_pool(name="products", bufs=4))
        norm_psum = ctx.enter_context(tc.psum_pool(name="norm_psum", bufs=1))
        ctx.enter_context(tc.manual_schedule())

        x_sb = keep.tile([P, D], BF16)
        nc.sync.dma_start(out=x_sb[:], in_=hidden_states.flatten_outer_dims())
        wa_sb = keep.tile([P, CHUNKS, D], BF16)
        wa_rows = kv_a_w_ckv.rearrange("(u p e) k -> u e p k", u=2, e=2)
        for t in range(CHUNKS):
            nc.sync.dma_start(out=wa_sb[:, t, :], in_=wa_rows[t // 2, t % 2])
        gain_bf = keep.tile([P, 2, 2], BF16)
        nc.sync.dma_start(out=gain_bf[:], in_=kv_a_ln_w.rearrange("(u p e) -> p u e", u=2, e=2))
        pe_sb = keep.tile([P, ROPE], BF16)
        for b in range(BATCH):
            nc.sync.dma_start(out=pe_sb[b:P:BATCH, :], in_=k_pe_raw[b])
        wb_sb = keep.tile([P, QUARTERS, PACK, KR], BF16)
        wb_rows = kv_b_w.rearrange("(q n i) k -> q n i k", q=QUARTERS, i=PACK)
        for q in range(QUARTERS):
            nc.sync.dma_start(out=wb_sb[:, q], in_=wb_rows[q])

        partition_no = keep.tile([P, 1], I32)
        nc.gpsimd.iota(partition_no[:], pattern=[[0, 1]], base=0, channel_multiplier=1)
        ident = keep.tile([P, P], F32)
        make_identity(nc, ident[:])
        ones = keep.tile([P, P], F32)
        nc.gpsimd.memset(ones[:], 1.0)

        freq = keep.tile([P, 2, ROPE_HALF], F32)
        nc.vector.memset(freq[:, :, 0:1], 1.0)
        for step in range(5):
            w = 2**step
            nc.vector.tensor_scalar(
                out=freq[:, :, w : 2 * w],
                in0=freq[:, :, 0:w],
                scalar1=THETA ** (-w / ROPE_HALF),
                scalar2=None,
                op0=ALU.mult,
            )
        eps = keep.tile([P, 1], F32)
        nc.vector.tensor_scalar(
            out=eps[:], in0=freq[:, 0, 0:1], scalar1=EPS, scalar2=None, op0=ALU.mult
        )
        pos_int = keep.tile([P, 1], I32)
        nc.vector.tensor_single_scalar(
            out=pos_int[:], in_=partition_no[:], scalar=1, op=ALU.arith_shift_right
        )
        pos = keep.tile([P, 1], F32)
        nc.vector.tensor_copy(out=pos[:], in_=pos_int[:])
        turns = keep.tile([P, 2, ROPE_HALF], F32)
        nc.vector.tensor_scalar(
            out=turns[:],
            in0=freq[:],
            scalar1=pos[:, 0:1],
            scalar2=1.0 / (2.0 * math.pi),
            op0=ALU.mult,
            op1=ALU.mult,
        )
        nc.vector.tensor_scalar_add(out=turns[:, 1, :], in0=turns[:, 1, :], scalar1=0.25)
        whole = keep.tile([P, 2, ROPE_HALF], F32)
        nc.vector.tensor_scalar(
            out=whole[:],
            in0=turns[:],
            scalar1=ROUND_MAGIC,
            scalar2=ROUND_MAGIC,
            op0=ALU.add,
            op1=ALU.subtract,
        )
        frac = keep.tile([P, 2, ROPE_HALF], F32)
        nc.vector.tensor_tensor(out=frac[:], in0=turns[:], in1=whole[:], op=ALU.subtract)
        sin_cos = keep.tile([P, 2, ROPE_HALF], F32)
        nc.scalar.activation(out=sin_cos[:], in_=frac[:], func=ACT.Sin, scale=2.0 * math.pi)
        table_warm = keep.tile([P, 1], F32)
        nc.scalar.activation(out=table_warm[:], in_=sin_cos[:, 1, 0:1], func=ACT.Abs_reciprocal_sqrt)

        gain = keep.tile([P, CHUNKS], F32)
        nc.gpsimd.tensor_copy(out=gain[:], in_=gain_bf[:].rearrange("p u e -> p (u e)"))
        prod = keep.tile([P, 2, 2, ROPE_HALF], F32)
        nc.gpsimd.tensor_tensor(
            out=prod[:],
            in0=pe_sb[:].rearrange("p (h j) -> p h j", h=2).unsqueeze(1).to_broadcast([P, 2, 2, ROPE_HALF]),
            in1=sin_cos[:].unsqueeze(2).to_broadcast([P, 2, 2, ROPE_HALF]),
            op=ALU.mult,
        )
        rope = keep.tile([P, ROPE], F32)
        nc.gpsimd.tensor_tensor(
            out=rope[:, 0:ROPE_HALF], in0=prod[:, 1, 0, :], in1=prod[:, 0, 1, :], op=ALU.subtract
        )
        nc.gpsimd.tensor_tensor(
            out=rope[:, ROPE_HALF:ROPE], in0=prod[:, 1, 1, :], in1=prod[:, 0, 0, :], op=ALU.add
        )
        for b in range(BATCH):
            nc.sync.dma_start(
                out=key_s[b].rearrange("h s d -> s h d")[:, :, HALF_HEAD:HEAD_COLS],
                in_=rope[b:P:BATCH, :].unsqueeze(1).to_broadcast([SEQ, HEADS, ROPE]),
            )

        x_grouped = keep.tile([P, PASSES_1, TOK, PACK], BF16, align_bytes=64)
        x_codes = keep.tile([P, PASSES_1, TOK], U32, align_bytes=64)
        x_scales = keep.tile([P, PASSES_1, TOK], U8, align_bytes=64)
        x_bank = staging.tile([P, PASSES_1, 2, TOK], F32, tag="bank")
        for g in range(PASSES_1):
            transpose_words(nc, x_bank[:, g], x_sb[:, K_PASS * g : K_PASS * (g + 1)], ident[:])
        for g in range(PASSES_1):
            nc.vector.tensor_copy(
                out=x_grouped[:, g].bitcast(F32).rearrange("p (s b) u -> p s b u", b=BATCH),
                in_=x_bank[:, g].rearrange("p u (b s) -> p s b u", b=BATCH),
            )

        wa_grouped = keep.tile([P, CHUNKS, PASSES_1, P, PACK], BF16, align_bytes=64)
        wa_codes = keep.tile([P, CHUNKS, PASSES_1, P], U32, align_bytes=64)
        wa_scales = keep.tile([P, CHUNKS, PASSES_1, P], U8, align_bytes=64)
        for t in range(CHUNKS):
            wa_bank = staging.tile([P, PASSES_1, 2, P], F32, tag="bank")
            for g in range(PASSES_1):
                transpose_words(
                    nc, wa_bank[:, g], wa_sb[:, t, K_PASS * g : K_PASS * (g + 1)], ident[:]
                )
            copy_out = nc.vector.tensor_copy if t == 0 else nc.scalar.copy
            copy_out(
                out=wa_grouped[:, t].bitcast(F32), in_=wa_bank[:].rearrange("p g u m -> p g m u")
            )
            if t == 0:
                quantise(
                    nc,
                    x_codes[:].rearrange("p g r -> p (g r)"),
                    x_scales[:].rearrange("p g r -> p (g r)"),
                    x_grouped[:].rearrange("p g r k -> p (g r k)"),
                )
            quantise(
                nc,
                wa_codes[:, t].rearrange("p g m -> p (g m)"),
                wa_scales[:, t].rearrange("p g m -> p (g m)"),
                wa_grouped[:, t].rearrange("p g m k -> p (g m k)"),
            )

        wb_grouped = keep.tile([P, WB_BANKS, BANK_ROWS, PACK], BF16, align_bytes=64)
        wb_codes = keep.tile([P, WB_BANKS, BANK_ROWS], U32, align_bytes=64)
        wb_scales = keep.tile([P, WB_BANKS, BANK_ROWS], U8, align_bytes=64)

        def transpose_and_regroup_wb(bank_no):
            wb_bank = staging.tile([P, 2, 2, P], F32, tag="bank")
            for j in range(2):
                rows = wb_sb[:, bank_no // 2, 2 * (bank_no % 2) + j, :]
                transpose_words(nc, wb_bank[:, j], rows, ident[:])
            copy_out = nc.vector.tensor_copy if bank_no == 0 else nc.scalar.copy
            copy_out(
                out=wb_grouped[:, bank_no].bitcast(F32).rearrange("p (j n) u -> p j n u", j=2),
                in_=wb_bank[:].rearrange("p j u n -> p j n u"),
            )

        def quantise_wb(bank_no):
            quantise(
                nc,
                wb_codes[:, bank_no, :],
                wb_scales[:, bank_no, :],
                wb_grouped[:, bank_no].rearrange("p c k -> p (c k)"),
            )

        squares = keep.tile([P, CHUNKS, TOK], F32)
        gained = keep.tile([P, CHUNKS, TOK], F32)

        def first_product(t):
            ckv_t = products.tile([P, TOK], F32, tag="product")
            for g in range(PASSES_1):
                nc.tensor.matmul_mx(
                    out=ckv_t[:],
                    lhsT=wa_codes[:, t, g, :].bitcast(FP8X4),
                    lhsT_scale=wa_scales[:, t, g, :],
                    rhs=x_codes[:, g, :].bitcast(FP8X4),
                    rhs_scale=x_scales[:, g, :],
                    start=(g == 0),
                    stop=(g == PASSES_1 - 1),
                )
            nc.scalar.activation(out=squares[:, t, :], in_=ckv_t[:], func=ACT.Square)
            nc.vector.tensor_scalar(
                out=gained[:, t, :], in0=ckv_t[:], scalar1=gain[:, t : t + 1], scalar2=None, op0=ALU.mult
            )

        first_product(0)
        first_product(1)
        squares_01 = keep.tile([P, TOK], F32)
        nc.vector.tensor_tensor(
            out=squares_01[:], in0=squares[:, 0, :], in1=squares[:, 1, :], op=ALU.add
        )
        first_product(2)
        squares_012 = keep.tile([P, TOK], F32)
        nc.vector.tensor_tensor(
            out=squares_012[:], in0=squares_01[:], in1=squares[:, 2, :], op=ALU.add
        )
        transpose_and_regroup_wb(0)
        first_product(3)
        quantise_wb(0)
        transpose_and_regroup_wb(1)

        sum_sq = norm_psum.tile([P, TOK], F32)
        nc.tensor.matmul(out=sum_sq[:], lhsT=ones[:], rhs=squares_012[:], start=True, stop=False)
        nc.tensor.matmul(out=sum_sq[:], lhsT=ones[:], rhs=squares[:, 3, :], start=False, stop=True)
        rstd = keep.tile([P, TOK], F32)
        nc.scalar.activation(
            out=rstd[:], in_=sum_sq[:], func=ACT.Abs_reciprocal_sqrt, bias=eps[:, 0:1], scale=1.0 / KR
        )
        quantise_wb(1)
        transpose_and_regroup_wb(2)
        cn_grouped = keep.tile([P, TOK, PACK], BF16, align_bytes=64)
        nc.vector.tensor_tensor(
            out=cn_grouped[:],
            in0=gained[:].rearrange("p t r -> p r t"),
            in1=rstd[:].unsqueeze(2).to_broadcast([P, TOK, PACK]),
            op=ALU.mult,
        )
        cn_codes = keep.tile([P, TOK], U32, align_bytes=64)
        cn_scales = keep.tile([P, TOK], U8, align_bytes=64)
        quantise(nc, cn_codes[:], cn_scales[:], cn_grouped[:].rearrange("p r k -> p (r k)"))
        quantise_wb(2)

        kv_sb = keep.tile([P, HEADS * HEAD_COLS], F32)

        def second_product(q):
            kv_ps = products.tile([P, QUARTER_COLS], F32, tag="product")
            nc.tensor.matmul_mx(
                out=kv_ps[:],
                lhsT=cn_codes[:].bitcast(FP8X4),
                lhsT_scale=cn_scales[:],
                rhs=wb_codes[:, 2 * q : 2 * q + 2, :].rearrange("p h c -> p (h c)").bitcast(FP8X4),
                rhs_scale=wb_scales[:, 2 * q : 2 * q + 2, :].rearrange("p h c -> p (h c)"),
                start=True,
                stop=True,
            )
            kv_cols = slice(QUARTER_COLS * q, QUARTER_COLS * (q + 1))
            copy_out = nc.scalar.copy if q == 2 else nc.vector.tensor_copy
            copy_out(
                out=kv_sb[:, kv_cols].rearrange("p (n i) -> p n i", i=PACK),
                in_=kv_ps[:].rearrange("p (i n) -> p n i", i=PACK),
            )
            heads = slice(HEADS_PER_QUARTER * q, HEADS_PER_QUARTER * (q + 1))
            for b in range(BATCH):
                by_head = kv_sb[b:P:BATCH, kv_cols].rearrange("s (h c) -> s h c", c=HEAD_COLS)
                nc.sync.dma_start(
                    out=key_s[b, heads, :, 0:HALF_HEAD].rearrange("h s d -> s h d"),
                    in_=by_head[:, :, 0:HALF_HEAD],
                )
                nc.sync.dma_start(
                    out=v[b, heads].rearrange("h s d -> s h d"),
                    in_=by_head[:, :, HALF_HEAD:HEAD_COLS],
                )

        for bank_no in range(3, WB_BANKS):
            transpose_and_regroup_wb(bank_no)
            if bank_no >= WB_BANKS - 3:
                second_product(bank_no - (WB_BANKS - 3))
            quantise_wb(bank_no)
        second_product(QUARTERS - 1)
